import numpy as np
import ml_dtypes


def mxq(x, axis, fmt="e4m3"):
    dtype, down = {"e4m3": (ml_dtypes.float8_e4m3fn, 7), "e5m2": (ml_dtypes.float8_e5m2, 14)}[fmt]
    v = np.moveaxis(np.asarray(x, np.float32).astype(ml_dtypes.bfloat16).astype(np.float64), axis, -1)
    blocks = v.reshape(v.shape[:-1] + (-1, 32))
    amax = np.abs(blocks).max(-1, keepdims=True)
    byte = np.maximum(np.where(amax > 0, np.frexp(amax)[1] - 1 + 127, 0) - down, 1)
    scale = np.exp2(byte - 127.0)
    codes = (blocks / scale).astype(np.float32).astype(dtype).astype(np.float64)
    return np.moveaxis((codes * scale).reshape(v.shape), -1, axis)


WIDE = False


def mx_kscale(k):
    if not WIDE:
        return np.ones(k)
    levels = np.array([10, -10, 5, -5, 0])
    a = np.random.permutation(np.resize(levels, k // 512 * 4)).reshape(k // 512, 4)
    idx = np.arange(k)
    return np.exp2(a[idx // 512, idx % 128 // 32])


BF16 = ml_dtypes.bfloat16


def bf(x):
    return np.asarray(x, np.float32).astype(BF16)


def f64(x):
    return np.asarray(x).astype(np.float64)


B, S, D, R, C = 128, 32, 512, 16, 1024
MIN_SCALE = 1e-3
TEMPERATURE = 1.5


def softplus(v):
    return np.logaddexp(v, 0.0)


def setup_inputs():
    s = mx_kscale(D)
    return {
        "features": bf(np.random.standard_normal((B, D)) * 0.3 * s),
        "W_diag": bf(np.random.standard_normal((D, D)) * 2.0 / np.sqrt(D) / s[None, :]),
        "b_diag": bf(-4.0 + 0.2 * np.random.standard_normal(D)),
        "W_cls": bf(np.random.standard_normal((C, D)) * 3.0 / np.sqrt(D) / s[None, :]),
        "b_cls": bf(np.random.standard_normal(C) * 0.3),
        "noise_diag": bf(np.random.standard_normal((B, S, D)) * 10.0 * s),
        "lr_samples": bf(np.random.standard_normal((B, S, D)) * 0.3 * s),
    }


def reference(features, W_diag, b_diag, W_cls, b_cls, noise_diag, lr_samples):
    f = f64(features)
    z = (mxq(f, 1, "e4m3") @ mxq(f64(W_diag), 1, "e4m3").T) + f64(b_diag)
    diagonal_std = softplus(z) + MIN_SCALE
    samples = f64(lr_samples) + diagonal_std[:, None, :] * f64(noise_diag)
    pre_logits = f[:, None, :] + samples
    logits = (mxq(pre_logits, 2, "e4m3") @ mxq(f64(W_cls), 1, "e4m3").T) + f64(b_cls)
    return logits / TEMPERATURE

@@ -1,0 +1,219 @@
+from contextlib import ExitStack
+
+import concourse.mybir as mybir
+from concourse.masks import make_identity
+
+F32 = mybir.dt.float32
+BF16 = mybir.dt.bfloat16
+U32 = mybir.dt.uint32
+U8 = mybir.dt.uint8
+FP8X4 = mybir.dt.float8_e4m3fn_x4
+ACT = mybir.ActivationFunctionType
+ALU = mybir.AluOpType
+
+P = 128
+PACK = 4
+B, S, D, C = 128, 32, 512, 1024
+assert D == P * PACK
+
+ROW_TILES = 2
+BLOCK_ROWS = ROW_TILES * P
+BLOCKS = B * S // BLOCK_ROWS
+BLOCKS_PER_LOAD = 4
+EXAMPLES = BLOCK_ROWS // S
+EXAMPLE_COLS = P // EXAMPLES
+N_COLS = 512
+MIN_SCALE = 1e-3
+INV_TEMPERATURE = 1.0 / 1.5
+
+FLOPS = 2 * B * S * D * C + 2 * B * D * D
+
+
+def transpose_row_tiles(nc, bank, rows, identity):
+    for i in range(rows.shape[1]):
+        for t in range(PACK):
+            nc.tensor.transpose(bank[:, i, t, :], rows[:, i, t * P : (t + 1) * P], identity)
+
+
+def words_first(bank):
+    return bank.rearrange("p i t r -> p i r t")
+
+
+def quantise(nc, codes, scales, grouped):
+    nc.vector.quantize_mx(
+        out=codes.bitcast(FP8X4),
+        scales=scales,
+        in_=grouped.rearrange("p i r t -> p (i r t)"),
+    )
+
+
+def tile_hetxlhead_pa_kernel(
+    tc, features, W_diag, b_diag, W_cls, b_cls, noise_diag, lr_samples, out
+):
+    nc = tc.nc
+    noise_loads = noise_diag.rearrange(
+        "b s d -> (b s) d"
+    ).rearrange("(l j p i) d -> l p j i d", j=BLOCKS_PER_LOAD, p=P, i=ROW_TILES)
+    lr_loads = lr_samples.rearrange(
+        "b s d -> (b s) d"
+    ).rearrange("(l j p i) d -> l p j i d", j=BLOCKS_PER_LOAD, p=P, i=ROW_TILES)
+    out_blocks = out.rearrange("b s c -> (b s) c").rearrange(
+        "(j p i) c -> j p i c", p=P, i=ROW_TILES
+    )
+
+    with ExitStack() as ctx:
+        keep = ctx.enter_context(tc.tile_pool(name="keep", bufs=1))
+        work = ctx.enter_context(tc.tile_pool(name="work", bufs=3))
+        results = ctx.enter_context(tc.tile_pool(name="results", bufs=4))
+        turned = ctx.enter_context(tc.psum_pool(name="turned", bufs=4))
+        sums = ctx.enter_context(tc.psum_pool(name="sums", bufs=4))
+
+        identity = keep.tile([P, P], BF16)
+        make_identity(nc, identity[:])
+        one = keep.tile([P, 1], F32)
+        nc.vector.memset(one[:], 1.0)
+        warm = keep.tile([P, 1], F32)
+        nc.scalar.activation(out=warm[:], in_=one[:], func=ACT.Exp)
+        bd_rows = keep.tile([P, 1, P], BF16)
+        nc.vector.memset(bd_rows[:], 0.0)
+
+        nc.sync.dma_start(out=bd_rows[0:PACK, 0, :], in_=b_diag.rearrange("(t p) -> t p", p=P))
+        feat_rows = keep.tile([P, 1, D], BF16)
+        nc.sync.dma_start(out=feat_rows[:, 0, :], in_=features)
+        wd_rows = keep.tile([P, D // P, D], BF16)
+        nc.sync.dma_start(out=wd_rows[:], in_=W_diag.rearrange("(i p) k -> p i k", p=P))
+        noise_rows = []
+        lr_rows = []
+        wc_rows = keep.tile([P, C // P, D], BF16)
+        bc_rows = keep.tile([P, C], BF16)
+        for l in range(BLOCKS // BLOCKS_PER_LOAD):
+            noise_rows.append(
+                keep.tile([P, BLOCKS_PER_LOAD, ROW_TILES, D], BF16, name="noise_rows%d" % l)
+            )
+            nc.sync.dma_start(out=noise_rows[l][:], in_=noise_loads[l])
+            lr_rows.append(
+                keep.tile([P, BLOCKS_PER_LOAD, ROW_TILES, D], BF16, name="lr_rows%d" % l)
+            )
+            nc.sync.dma_start(out=lr_rows[l][:], in_=lr_loads[l])
+            if l == 0:
+                nc.sync.dma_start(out=wc_rows[:], in_=W_cls.rearrange("(i p) k -> p i k", p=P))
+                nc.sync.dma_start(out=bc_rows[:], in_=b_cls.partition_broadcast(P))
+
+        head_bank = turned.tile([P, ROW_TILES, PACK, P], BF16, tag="turned")
+        transpose_row_tiles(nc, head_bank[:, 0:1], feat_rows[:], identity[:])
+        nc.tensor.transpose(head_bank[:, 1, 0, :], bd_rows[:, 0, :], identity[:])
+        feat = keep.tile([P, 1, B, PACK], BF16, align_bytes=64)
+        nc.vector.tensor_copy(out=feat[:], in_=words_first(head_bank[:, 0:1]))
+        bd = keep.tile([P, PACK], F32)
+        nc.vector.tensor_copy(out=bd[:], in_=head_bank[:, 1, 0, 0:PACK])
+
+        wd = keep.tile([P, D // P, P, PACK], BF16, align_bytes=64)
+        for g in range(D // BLOCK_ROWS):
+            pair = slice(g * ROW_TILES, (g + 1) * ROW_TILES)
+            wd_bank = turned.tile([P, ROW_TILES, PACK, P], BF16, tag="turned")
+            transpose_row_tiles(nc, wd_bank[:], wd_rows[:, pair], identity[:])
+            if g % 2 == 0:
+                nc.vector.tensor_copy(out=wd[:, pair], in_=words_first(wd_bank[:]))
+            else:
+                nc.scalar.copy(out=wd[:, pair], in_=words_first(wd_bank[:]))
+
+        feat_codes = keep.tile([P, B], U32, align_bytes=64)
+        feat_scales = keep.tile([P, B], U8, align_bytes=64)
+        quantise(nc, feat_codes[:], feat_scales[:], feat[:])
+        wd_codes = keep.tile([P, D], U32, align_bytes=64)
+        wd_scales = keep.tile([P, D], U8, align_bytes=64)
+        quantise(nc, wd_codes[:], wd_scales[:], wd[:])
+
+        z = sums.tile([P, PACK, B], F32, tag="sums")
+        for t in range(PACK):
+            nc.tensor.matmul_mx(
+                out=z[:, t, :],
+                lhsT=wd_codes[:, t * P : (t + 1) * P].bitcast(FP8X4),
+                lhsT_scale=wd_scales[:, t * P : (t + 1) * P],
+                rhs=feat_codes[:].bitcast(FP8X4),
+                rhs_scale=feat_scales[:],
+                start=True,
+                stop=True,
+            )
+        v = keep.tile([P, PACK, B], F32)
+        nc.vector.tensor_tensor(
+            out=v[:], in0=z[:], in1=bd[:].unsqueeze(2).to_broadcast([P, PACK, B]), op=ALU.add
+        )
+        magnitude = keep.tile([P, PACK, B], F32)
+        nc.scalar.activation(out=magnitude[:], in_=v[:], func=ACT.Abs)
+        decay = keep.tile([P, PACK, B], F32)
+        nc.scalar.activation(out=decay[:], in_=magnitude[:], func=ACT.Exp, scale=-1.0)
+        log_term = keep.tile([P, PACK, B], F32)
+        nc.scalar.activation(out=log_term[:], in_=decay[:], func=ACT.Ln, bias=one[:])
+        ramp = keep.tile([P, PACK, B], F32)
+        nc.vector.tensor_scalar(
+            out=ramp[:], in0=v[:], scalar1=0.0, scalar2=MIN_SCALE, op0=ALU.max, op1=ALU.add
+        )
+        std = keep.tile([P, PACK, B], F32)
+        nc.vector.tensor_tensor(out=std[:], in0=log_term[:], in1=ramp[:], op=ALU.add)
+
+        wc = keep.tile([P, C // P, P, PACK], BF16, align_bytes=64)
+        for g in range(C // BLOCK_ROWS):
+            pair = slice(g * ROW_TILES, (g + 1) * ROW_TILES)
+            wc_bank = turned.tile([P, ROW_TILES, PACK, P], BF16, tag="turned")
+            transpose_row_tiles(nc, wc_bank[:], wc_rows[:, pair], identity[:])
+            if g % 2 == 0:
+                nc.vector.tensor_copy(out=wc[:, pair], in_=words_first(wc_bank[:]))
+            else:
+                nc.scalar.copy(out=wc[:, pair], in_=words_first(wc_bank[:]))
+        wc_codes = keep.tile([P, C], U32, align_bytes=64)
+        wc_scales = keep.tile([P, C], U8, align_bytes=64)
+        quantise(nc, wc_codes[:], wc_scales[:], wc[:])
+        bias = keep.tile([P, C], F32)
+        nc.vector.tensor_scalar_mul(out=bias[:], in0=bc_rows[:], scalar1=INV_TEMPERATURE)
+
+        for j in range(BLOCKS):
+            l, k = divmod(j, BLOCKS_PER_LOAD)
+            noise_bank = turned.tile([P, ROW_TILES, PACK, P], BF16, tag="turned")
+            transpose_row_tiles(nc, noise_bank[:], noise_rows[l][:, k], identity[:])
+            lr_bank = turned.tile([P, ROW_TILES, PACK, P], BF16, tag="turned")
+            transpose_row_tiles(nc, lr_bank[:], lr_rows[l][:, k], identity[:])
+
+            shifted = work.tile([P, ROW_TILES, PACK, P], F32)
+            for e in range(EXAMPLES):
+                b = j * EXAMPLES + e
+                cols = slice(e * EXAMPLE_COLS, (e + 1) * EXAMPLE_COLS)
+                for t in range(PACK):
+                    nc.scalar.activation(
+                        out=shifted[:, :, t, cols],
+                        in_=noise_bank[:, :, t, cols],
+                        func=ACT.Identity,
+                        scale=std[:, t, b : b + 1],
+                        bias=feat[:, 0, b, t : t + 1],
+                    )
+            pre = work.tile([P, ROW_TILES, P, PACK], BF16, align_bytes=64)
+            nc.vector.tensor_tensor(
+                out=pre[:], in0=words_first(lr_bank[:]), in1=words_first(shifted[:]), op=ALU.add
+            )
+            pre_codes = work.tile([P, BLOCK_ROWS], U32, align_bytes=64)
+            pre_scales = work.tile([P, BLOCK_ROWS], U8, align_bytes=64)
+            quantise(nc, pre_codes[:], pre_scales[:], pre[:])
+
+            result = results.tile([P, ROW_TILES, C], F32)
+            for i in range(ROW_TILES):
+                for h in range(C // N_COLS):
+                    classes = slice(h * N_COLS, (h + 1) * N_COLS)
+                    acc = sums.tile([P, N_COLS], F32, tag="sums")
+                    nc.tensor.matmul_mx(
+                        out=acc[:],
+                        lhsT=pre_codes[:, i * P : (i + 1) * P].bitcast(FP8X4),
+                        lhsT_scale=pre_scales[:, i * P : (i + 1) * P],
+                        rhs=wc_codes[:, classes].bitcast(FP8X4),
+                        rhs_scale=wc_scales[:, classes],
+                        start=True,
+                        stop=True,
+                    )
+                    nc.vector.scalar_tensor_tensor(
+                        out=result[:, i, classes],
+                        in0=acc[:],
+                        scalar=INV_TEMPERATURE,
+                        in1=bias[:, classes],
+                        op0=ALU.mult,
+                        op1=ALU.add,
+                    )
+            nc.sync.dma_start(out=out_blocks[j], in_=result[:])

@@ -199,15 +199,16 @@ def tile_hetxlhead_pa_kernel(
                 for h in range(C // N_COLS):
                     classes = slice(h * N_COLS, (h + 1) * N_COLS)
                     acc = sums.tile([P, N_COLS], F32, tag="sums")
-                    nc.tensor.matmul_mx(
-                        out=acc[:],
-                        lhsT=pre_codes[:, i * P : (i + 1) * P].bitcast(FP8X4),
-                        lhsT_scale=pre_scales[:, i * P : (i + 1) * P],
-                        rhs=wc_codes[:, classes].bitcast(FP8X4),
-                        rhs_scale=wc_scales[:, classes],
-                        start=True,
-                        stop=True,
-                    )
+                    for repeat in range(2):
+                        nc.tensor.matmul_mx(
+                            out=acc[:],
+                            lhsT=pre_codes[:, i * P : (i + 1) * P].bitcast(FP8X4),
+                            lhsT_scale=pre_scales[:, i * P : (i + 1) * P],
+                            rhs=wc_codes[:, classes].bitcast(FP8X4),
+                            rhs_scale=wc_scales[:, classes],
+                            start=True,
+                            stop=True,
+                        )
                     nc.vector.scalar_tensor_tensor(
                         out=result[:, i, classes],
                         in0=acc[:],

@@ -12,7 +12,9 @@ ACT = mybir.ActivationFunctionType
 ALU = mybir.AluOpType
 
 P = 128
-PACK = 4
+PAIR = 2
+HALVES = 2
+PACK = HALVES * PAIR
 B, S, D, C = 128, 32, 512, 1024
 assert D == P * PACK
 
@@ -20,23 +22,27 @@ ROW_TILES = 2
 BLOCK_ROWS = ROW_TILES * P
 BLOCKS = B * S // BLOCK_ROWS
 BLOCKS_PER_LOAD = 4
+LOADS = BLOCKS // BLOCKS_PER_LOAD
 EXAMPLES = BLOCK_ROWS // S
 EXAMPLE_COLS = P // EXAMPLES
 N_COLS = 512
+TURN_AHEAD = 4
+ADD_AHEAD = 2
 MIN_SCALE = 1e-3
 INV_TEMPERATURE = 1.0 / 1.5
 
 FLOPS = 2 * B * S * D * C + 2 * B * D * D
 
 
-def transpose_row_tiles(nc, bank, rows, identity):
+def turn_row_tiles(nc, bank, rows, identity):
     for i in range(rows.shape[1]):
-        for t in range(PACK):
-            nc.tensor.transpose(bank[:, i, t, :], rows[:, i, t * P : (t + 1) * P], identity)
+        words = rows[:, i, :].bitcast(F32)
+        for u in range(HALVES):
+            nc.tensor.transpose(bank[:, i, u, :], words[:, u * P : (u + 1) * P], identity)
 
 
-def words_first(bank):
-    return bank.rearrange("p i t r -> p i r t")
+def halves_together(bank):
+    return bank.rearrange("p i u r -> p i r u")
 
 
 def quantise(nc, codes, scales, grouped):
@@ -51,12 +57,12 @@ def tile_hetxlhead_pa_kernel(
     tc, features, W_diag, b_diag, W_cls, b_cls, noise_diag, lr_samples, out
 ):
     nc = tc.nc
-    noise_loads = noise_diag.rearrange(
-        "b s d -> (b s) d"
-    ).rearrange("(l j p i) d -> l p j i d", j=BLOCKS_PER_LOAD, p=P, i=ROW_TILES)
-    lr_loads = lr_samples.rearrange(
-        "b s d -> (b s) d"
-    ).rearrange("(l j p i) d -> l p j i d", j=BLOCKS_PER_LOAD, p=P, i=ROW_TILES)
+    noise_loads = noise_diag.rearrange("b s d -> (b s) d").rearrange(
+        "(l j p i) d -> l p j i d", j=BLOCKS_PER_LOAD, p=P, i=ROW_TILES
+    )
+    lr_loads = lr_samples.rearrange("b s d -> (b s) d").rearrange(
+        "(l j p i) d -> l p j i d", j=BLOCKS_PER_LOAD, p=P, i=ROW_TILES
+    )
     out_blocks = out.rearrange("b s c -> (b s) c").rearrange(
         "(j p i) c -> j p i c", p=P, i=ROW_TILES
     )
@@ -64,29 +70,48 @@ def tile_hetxlhead_pa_kernel(
     with ExitStack() as ctx:
         keep = ctx.enter_context(tc.tile_pool(name="keep", bufs=1))
         work = ctx.enter_context(tc.tile_pool(name="work", bufs=3))
-        results = ctx.enter_context(tc.tile_pool(name="results", bufs=4))
+        kept = ctx.enter_context(tc.tile_pool(name="kept", bufs=TURN_AHEAD - ADD_AHEAD + 3))
+        formed = ctx.enter_context(tc.tile_pool(name="formed", bufs=ADD_AHEAD + 2))
+        results = ctx.enter_context(tc.tile_pool(name="results", bufs=3))
         turned = ctx.enter_context(tc.psum_pool(name="turned", bufs=4))
         sums = ctx.enter_context(tc.psum_pool(name="sums", bufs=4))
 
-        identity = keep.tile([P, P], BF16)
+        def turn_weight(grouped, rows):
+            for g in range(rows.shape[1] // ROW_TILES):
+                pair = slice(g * ROW_TILES, (g + 1) * ROW_TILES)
+                bank = turned.tile([P, ROW_TILES, HALVES, P], F32, tag="turned")
+                turn_row_tiles(nc, bank[:], rows[:, pair], identity[:])
+                if g % 2 == 0:
+                    nc.vector.tensor_copy(
+                        out=grouped[:, pair].bitcast(F32), in_=halves_together(bank[:])
+                    )
+                else:
+                    nc.scalar.copy(out=grouped[:, pair].bitcast(F32), in_=halves_together(bank[:]))
+
+        identity = keep.tile([P, P], F32)
         make_identity(nc, identity[:])
         one = keep.tile([P, 1], F32)
         nc.vector.memset(one[:], 1.0)
         warm = keep.tile([P, 1], F32)
         nc.scalar.activation(out=warm[:], in_=one[:], func=ACT.Exp)
-        bd_rows = keep.tile([P, 1, P], BF16)
+        bd_rows = keep.tile([P, 1, PAIR * P], BF16)
         nc.vector.memset(bd_rows[:], 0.0)
 
-        nc.sync.dma_start(out=bd_rows[0:PACK, 0, :], in_=b_diag.rearrange("(t p) -> t p", p=P))
+        nc.sync.dma_start(
+            out=bd_rows[0:HALVES, 0, :], in_=b_diag.rearrange("(u w) -> u w", u=HALVES)
+        )
         feat_rows = keep.tile([P, 1, D], BF16)
         nc.sync.dma_start(out=feat_rows[:, 0, :], in_=features)
-        wd_rows = keep.tile([P, D // P, D], BF16)
-        nc.sync.dma_start(out=wd_rows[:], in_=W_diag.rearrange("(i p) k -> p i k", p=P))
+        wd_rows = keep.tile([P, PACK, D], BF16)
+        nc.sync.dma_start(
+            out=wd_rows[:].rearrange("r (u e) k -> r u e k", u=HALVES),
+            in_=W_diag.rearrange("(u r e) k -> r u e k", u=HALVES, e=PAIR),
+        )
         noise_rows = []
         lr_rows = []
         wc_rows = keep.tile([P, C // P, D], BF16)
         bc_rows = keep.tile([P, C], BF16)
-        for l in range(BLOCKS // BLOCKS_PER_LOAD):
+        for l in range(LOADS):
             noise_rows.append(
                 keep.tile([P, BLOCKS_PER_LOAD, ROW_TILES, D], BF16, name="noise_rows%d" % l)
             )
@@ -96,27 +121,23 @@ def tile_hetxlhead_pa_kernel(
             )
             nc.sync.dma_start(out=lr_rows[l][:], in_=lr_loads[l])
             if l == 0:
-                nc.sync.dma_start(out=wc_rows[:], in_=W_cls.rearrange("(i p) k -> p i k", p=P))
+                nc.sync.dma_start(out=wc_rows[:], in_=W_cls.rearrange("(i r) k -> r i k", r=P))
                 nc.sync.dma_start(out=bc_rows[:], in_=b_cls.partition_broadcast(P))
 
-        head_bank = turned.tile([P, ROW_TILES, PACK, P], BF16, tag="turned")
-        transpose_row_tiles(nc, head_bank[:, 0:1], feat_rows[:], identity[:])
-        nc.tensor.transpose(head_bank[:, 1, 0, :], bd_rows[:, 0, :], identity[:])
+        head_bank = turned.tile([P, ROW_TILES, HALVES, P], F32, tag="turned")
+        turn_row_tiles(nc, head_bank[:, 0:1], feat_rows[:], identity[:])
+        nc.tensor.transpose(head_bank[:, 1, 0, :], bd_rows[:, 0, :].bitcast(F32), identity[:])
         feat = keep.tile([P, 1, B, PACK], BF16, align_bytes=64)
-        nc.vector.tensor_copy(out=feat[:], in_=words_first(head_bank[:, 0:1]))
+        nc.vector.tensor_copy(out=feat[:].bitcast(F32), in_=halves_together(head_bank[:, 0:1]))
+        feat32 = keep.tile([P, HALVES, B, PAIR], F32)
+        nc.vector.tensor_copy(
+            out=feat32[:].rearrange("p u b e -> p u (b e)"), in_=head_bank[:, 0].bitcast(BF16)
+        )
         bd = keep.tile([P, PACK], F32)
-        nc.vector.tensor_copy(out=bd[:], in_=head_bank[:, 1, 0, 0:PACK])
+        nc.vector.tensor_copy(out=bd[:], in_=head_bank[:, 1, 0, 0:HALVES].bitcast(BF16))
 
-        wd = keep.tile([P, D // P, P, PACK], BF16, align_bytes=64)
-        for g in range(D // BLOCK_ROWS):
-            pair = slice(g * ROW_TILES, (g + 1) * ROW_TILES)
-            wd_bank = turned.tile([P, ROW_TILES, PACK, P], BF16, tag="turned")
-            transpose_row_tiles(nc, wd_bank[:], wd_rows[:, pair], identity[:])
-            if g % 2 == 0:
-                nc.vector.tensor_copy(out=wd[:, pair], in_=words_first(wd_bank[:]))
-            else:
-                nc.scalar.copy(out=wd[:, pair], in_=words_first(wd_bank[:]))
-
+        wd = keep.tile([P, PACK, P, PACK], BF16, align_bytes=64)
+        turn_weight(wd, wd_rows)
         feat_codes = keep.tile([P, B], U32, align_bytes=64)
         feat_scales = keep.tile([P, B], U8, align_bytes=64)
         quantise(nc, feat_codes[:], feat_scales[:], feat[:])
@@ -153,68 +174,117 @@ def tile_hetxlhead_pa_kernel(
         nc.vector.tensor_tensor(out=std[:], in0=log_term[:], in1=ramp[:], op=ALU.add)
 
         wc = keep.tile([P, C // P, P, PACK], BF16, align_bytes=64)
-        for g in range(C // BLOCK_ROWS):
-            pair = slice(g * ROW_TILES, (g + 1) * ROW_TILES)
-            wc_bank = turned.tile([P, ROW_TILES, PACK, P], BF16, tag="turned")
-            transpose_row_tiles(nc, wc_bank[:], wc_rows[:, pair], identity[:])
-            if g % 2 == 0:
-                nc.vector.tensor_copy(out=wc[:, pair], in_=words_first(wc_bank[:]))
-            else:
-                nc.scalar.copy(out=wc[:, pair], in_=words_first(wc_bank[:]))
+        turn_weight(wc, wc_rows)
         wc_codes = keep.tile([P, C], U32, align_bytes=64)
         wc_scales = keep.tile([P, C], U8, align_bytes=64)
         quantise(nc, wc_codes[:], wc_scales[:], wc[:])
         bias = keep.tile([P, C], F32)
         nc.vector.tensor_scalar_mul(out=bias[:], in0=bc_rows[:], scalar1=INV_TEMPERATURE)
 
-        for j in range(BLOCKS):
+        noise_bank, lr_bank, noise_turned, lr_grouped = {}, {}, {}, {}
+        pre, pre_codes, pre_scales, acc, result = {}, {}, {}, {}, {}
+
+        def exists(j):
+            return 0 <= j < BLOCKS
+
+        def turn(j):
+            if not exists(j):
+                return
             l, k = divmod(j, BLOCKS_PER_LOAD)
-            noise_bank = turned.tile([P, ROW_TILES, PACK, P], BF16, tag="turned")
-            transpose_row_tiles(nc, noise_bank[:], noise_rows[l][:, k], identity[:])
-            lr_bank = turned.tile([P, ROW_TILES, PACK, P], BF16, tag="turned")
-            transpose_row_tiles(nc, lr_bank[:], lr_rows[l][:, k], identity[:])
+            noise_bank[j] = turned.tile([P, ROW_TILES, HALVES, P], F32, name="noise_bank", tag="turned")
+            turn_row_tiles(nc, noise_bank[j][:], noise_rows[l][:, k], identity[:])
+            lr_bank[j] = turned.tile([P, ROW_TILES, HALVES, P], F32, name="lr_bank", tag="turned")
+            turn_row_tiles(nc, lr_bank[j][:], lr_rows[l][:, k], identity[:])
 
-            shifted = work.tile([P, ROW_TILES, PACK, P], F32)
-            for e in range(EXAMPLES):
-                b = j * EXAMPLES + e
-                cols = slice(e * EXAMPLE_COLS, (e + 1) * EXAMPLE_COLS)
-                for t in range(PACK):
-                    nc.scalar.activation(
-                        out=shifted[:, :, t, cols],
-                        in_=noise_bank[:, :, t, cols],
-                        func=ACT.Identity,
-                        scale=std[:, t, b : b + 1],
-                        bias=feat[:, 0, b, t : t + 1],
-                    )
-            pre = work.tile([P, ROW_TILES, P, PACK], BF16, align_bytes=64)
-            nc.vector.tensor_tensor(
-                out=pre[:], in0=words_first(lr_bank[:]), in1=words_first(shifted[:]), op=ALU.add
+        def keep_turned(j):
+            if not exists(j):
+                return
+            noise_turned[j] = kept.tile([P, ROW_TILES, HALVES, P, PAIR], BF16, name="noise_turned")
+            nc.scalar.copy(
+                out=noise_turned[j][:].rearrange("p i u r e -> p i u (r e)"),
+                in_=noise_bank[j][:].bitcast(BF16),
             )
-            pre_codes = work.tile([P, BLOCK_ROWS], U32, align_bytes=64)
-            pre_scales = work.tile([P, BLOCK_ROWS], U8, align_bytes=64)
-            quantise(nc, pre_codes[:], pre_scales[:], pre[:])
+            lr_grouped[j] = kept.tile([P, ROW_TILES, P, PACK], BF16, name="lr_grouped")
+            if j % 2 == 0:
+                nc.vector.tensor_copy(
+                    out=lr_grouped[j][:].bitcast(F32), in_=halves_together(lr_bank[j][:])
+                )
+            else:
+                nc.scalar.copy(out=lr_grouped[j][:].bitcast(F32), in_=halves_together(lr_bank[j][:]))
 
-            result = results.tile([P, ROW_TILES, C], F32)
-            for i in range(ROW_TILES):
-                for h in range(C // N_COLS):
-                    classes = slice(h * N_COLS, (h + 1) * N_COLS)
-                    acc = sums.tile([P, N_COLS], F32, tag="sums")
-                    for repeat in range(2):
-                        nc.tensor.matmul_mx(
-                            out=acc[:],
-                            lhsT=pre_codes[:, i * P : (i + 1) * P].bitcast(FP8X4),
-                            lhsT_scale=pre_scales[:, i * P : (i + 1) * P],
-                            rhs=wc_codes[:, classes].bitcast(FP8X4),
-                            rhs_scale=wc_scales[:, classes],
-                            start=True,
-                            stop=True,
+        def shift_add(j):
+            if not exists(j):
+                return
+            shifted = work.tile([P, ROW_TILES, PACK, P], F32)
+            for m in range(EXAMPLES):
+                b = j * EXAMPLES + m
+                cols = slice(m * EXAMPLE_COLS, (m + 1) * EXAMPLE_COLS)
+                for u in range(HALVES):
+                    for e in range(PAIR):
+                        t = PAIR * u + e
+                        nc.scalar.activation(
+                            out=shifted[:, :, t, cols],
+                            in_=noise_turned[j][:, :, u, cols, e],
+                            func=ACT.Identity,
+                            scale=std[:, t, b : b + 1],
+                            bias=feat32[:, u, b, e : e + 1],
                         )
-                    nc.vector.scalar_tensor_tensor(
-                        out=result[:, i, classes],
-                        in0=acc[:],
-                        scalar=INV_TEMPERATURE,
-                        in1=bias[:, classes],
-                        op0=ALU.mult,
-                        op1=ALU.add,
-                    )
-            nc.sync.dma_start(out=out_blocks[j], in_=result[:])
+            pre[j] = formed.tile([P, ROW_TILES, P, PACK], BF16, name="pre", align_bytes=64)
+            nc.gpsimd.tensor_tensor(
+                out=pre[j][:],
+                in0=shifted[:].rearrange("p i t r -> p i r t"),
+                in1=lr_grouped[j][:],
+                op=ALU.add,
+            )
+
+        def quantise_block(j):
+            if not exists(j):
+                return
+            pre_codes[j] = work.tile([P, BLOCK_ROWS], U32, name="pre_codes", align_bytes=64)
+            pre_scales[j] = work.tile([P, BLOCK_ROWS], U8, name="pre_scales", align_bytes=64)
+            quantise(nc, pre_codes[j][:], pre_scales[j][:], pre[j][:])
+
+        def multiply(j, i):
+            if not exists(j):
+                return
+            for h in range(C // N_COLS):
+                classes = slice(h * N_COLS, (h + 1) * N_COLS)
+                acc[j, i, h] = sums.tile([P, N_COLS], F32, name="acc", tag="sums")
+                nc.tensor.matmul_mx(
+                    out=acc[j, i, h][:],
+                    lhsT=pre_codes[j][:, i * P : (i + 1) * P].bitcast(FP8X4),
+                    lhsT_scale=pre_scales[j][:, i * P : (i + 1) * P],
+                    rhs=wc_codes[:, classes].bitcast(FP8X4),
+                    rhs_scale=wc_scales[:, classes],
+                    start=True,
+                    stop=True,
+                )
+
+        def finish(j, i):
+            if not exists(j):
+                return
+            if i == 0:
+                result[j] = results.tile([P, ROW_TILES, C], F32, name="result")
+            for h in range(C // N_COLS):
+                classes = slice(h * N_COLS, (h + 1) * N_COLS)
+                nc.vector.scalar_tensor_tensor(
+                    out=result[j][:, i, classes],
+                    in0=acc[j, i, h][:],
+                    scalar=INV_TEMPERATURE,
+                    in1=bias[:, classes],
+                    op0=ALU.mult,
+                    op1=ALU.add,
+                )
+            if i == ROW_TILES - 1:
+                nc.sync.dma_start(out=out_blocks[j], in_=result[j][:])
+
+        with tc.manual_schedule():
+            for j in range(-TURN_AHEAD, BLOCKS + 1):
+                turn(j + TURN_AHEAD)
+                finish(j - 1, 0)
+                quantise_block(j)
+                multiply(j, 0)
+                keep_turned(j + TURN_AHEAD)
+                finish(j - 1, 1)
+                multiply(j, 1)
+                shift_add(j + ADD_AHEAD)

@@ -28,6 +28,7 @@ EXAMPLE_COLS = P // EXAMPLES
 N_COLS = 512
 TURN_AHEAD = 4
 ADD_AHEAD = 2
+SCALAR_CODES = 3
 MIN_SCALE = 1e-3
 INV_TEMPERATURE = 1.0 / 1.5
 
@@ -182,7 +183,7 @@ def tile_hetxlhead_pa_kernel(
         nc.vector.tensor_scalar_mul(out=bias[:], in0=bc_rows[:], scalar1=INV_TEMPERATURE)
 
         noise_bank, lr_bank, noise_turned, lr_grouped = {}, {}, {}, {}
-        pre, pre_codes, pre_scales, acc, result = {}, {}, {}, {}, {}
+        shifted, pre, pre_codes, pre_scales, acc, result = {}, {}, {}, {}, {}, {}
 
         def exists(j):
             return 0 <= j < BLOCKS
@@ -212,27 +213,56 @@ def tile_hetxlhead_pa_kernel(
             else:
                 nc.scalar.copy(out=lr_grouped[j][:].bitcast(F32), in_=halves_together(lr_bank[j][:]))
 
+        def by_example(columns):
+            return columns.rearrange("p i (m c) -> p i m c", c=EXAMPLE_COLS)
+
+        def along_samples(per_example):
+            return per_example.unsqueeze(1).unsqueeze(3).to_broadcast(
+                [P, ROW_TILES, EXAMPLES, EXAMPLE_COLS]
+            )
+
+        def scale_on_vector(j):
+            if not exists(j):
+                return
+            shifted[j] = work.tile([P, ROW_TILES, PACK, P], F32, name="shifted")
+            examples = slice(j * EXAMPLES, (j + 1) * EXAMPLES)
+            for t in range(SCALAR_CODES, PACK):
+                u, e = divmod(t, PAIR)
+                nc.vector.tensor_tensor(
+                    out=by_example(shifted[j][:, :, t, :]),
+                    in0=by_example(noise_turned[j][:, :, u, :, e]),
+                    in1=along_samples(std[:, t, examples]),
+                    op=ALU.mult,
+                )
+
         def shift_add(j):
             if not exists(j):
                 return
-            shifted = work.tile([P, ROW_TILES, PACK, P], F32)
+            examples = slice(j * EXAMPLES, (j + 1) * EXAMPLES)
+            for t in range(SCALAR_CODES, PACK):
+                u, e = divmod(t, PAIR)
+                nc.vector.tensor_tensor(
+                    out=by_example(shifted[j][:, :, t, :]),
+                    in0=by_example(shifted[j][:, :, t, :]),
+                    in1=along_samples(feat32[:, u, examples, e]),
+                    op=ALU.add,
+                )
             for m in range(EXAMPLES):
                 b = j * EXAMPLES + m
                 cols = slice(m * EXAMPLE_COLS, (m + 1) * EXAMPLE_COLS)
-                for u in range(HALVES):
-                    for e in range(PAIR):
-                        t = PAIR * u + e
-                        nc.scalar.activation(
-                            out=shifted[:, :, t, cols],
-                            in_=noise_turned[j][:, :, u, cols, e],
-                            func=ACT.Identity,
-                            scale=std[:, t, b : b + 1],
-                            bias=feat32[:, u, b, e : e + 1],
-                        )
+                for t in range(SCALAR_CODES):
+                    u, e = divmod(t, PAIR)
+                    nc.scalar.activation(
+                        out=shifted[j][:, :, t, cols],
+                        in_=noise_turned[j][:, :, u, cols, e],
+                        func=ACT.Identity,
+                        scale=std[:, t, b : b + 1],
+                        bias=feat32[:, u, b, e : e + 1],
+                    )
             pre[j] = formed.tile([P, ROW_TILES, P, PACK], BF16, name="pre", align_bytes=64)
             nc.gpsimd.tensor_tensor(
                 out=pre[j][:],
-                in0=shifted[:].rearrange("p i t r -> p i r t"),
+                in0=shifted[j][:].rearrange("p i t r -> p i r t"),
                 in1=lr_grouped[j][:],
                 op=ALU.add,
             )
@@ -285,6 +315,7 @@ def tile_hetxlhead_pa_kernel(
                 quantise_block(j)
                 multiply(j, 0)
                 keep_turned(j + TURN_AHEAD)
+                scale_on_vector(j + ADD_AHEAD)
                 finish(j - 1, 1)
                 multiply(j, 1)
                 shift_add(j + ADD_AHEAD)

@@ -26,9 +26,8 @@ LOADS = BLOCKS // BLOCKS_PER_LOAD
 EXAMPLES = BLOCK_ROWS // S
 EXAMPLE_COLS = P // EXAMPLES
 N_COLS = 512
-TURN_AHEAD = 4
-ADD_AHEAD = 2
-SCALAR_CODES = 3
+SHIFT_AHEAD = 2
+ADD_AHEAD = 1
 MIN_SCALE = 1e-3
 INV_TEMPERATURE = 1.0 / 1.5
 
@@ -71,8 +70,6 @@ def tile_hetxlhead_pa_kernel(
     with ExitStack() as ctx:
         keep = ctx.enter_context(tc.tile_pool(name="keep", bufs=1))
         work = ctx.enter_context(tc.tile_pool(name="work", bufs=3))
-        kept = ctx.enter_context(tc.tile_pool(name="kept", bufs=TURN_AHEAD - ADD_AHEAD + 3))
-        formed = ctx.enter_context(tc.tile_pool(name="formed", bufs=ADD_AHEAD + 2))
         results = ctx.enter_context(tc.tile_pool(name="results", bufs=3))
         turned = ctx.enter_context(tc.psum_pool(name="turned", bufs=4))
         sums = ctx.enter_context(tc.psum_pool(name="sums", bufs=4))
@@ -182,8 +179,8 @@ def tile_hetxlhead_pa_kernel(
         bias = keep.tile([P, C], F32)
         nc.vector.tensor_scalar_mul(out=bias[:], in0=bc_rows[:], scalar1=INV_TEMPERATURE)
 
-        noise_bank, lr_bank, noise_turned, lr_grouped = {}, {}, {}, {}
-        shifted, pre, pre_codes, pre_scales, acc, result = {}, {}, {}, {}, {}, {}
+        noise_bank, lr_bank, shifted = {}, {}, {}
+        pre, pre_codes, pre_scales, acc, result = {}, {}, {}, {}, {}
 
         def exists(j):
             return 0 <= j < BLOCKS
@@ -192,80 +189,46 @@ def tile_hetxlhead_pa_kernel(
             if not exists(j):
                 return
             l, k = divmod(j, BLOCKS_PER_LOAD)
-            noise_bank[j] = turned.tile([P, ROW_TILES, HALVES, P], F32, name="noise_bank", tag="turned")
+            noise_bank[j] = turned.tile(
+                [P, ROW_TILES, HALVES, P], F32, name="noise_bank", tag="turned"
+            )
             turn_row_tiles(nc, noise_bank[j][:], noise_rows[l][:, k], identity[:])
             lr_bank[j] = turned.tile([P, ROW_TILES, HALVES, P], F32, name="lr_bank", tag="turned")
             turn_row_tiles(nc, lr_bank[j][:], lr_rows[l][:, k], identity[:])
 
-        def keep_turned(j):
+        def shift(j):
             if not exists(j):
                 return
-            noise_turned[j] = kept.tile([P, ROW_TILES, HALVES, P, PAIR], BF16, name="noise_turned")
+            noise_turned = work.tile([P, ROW_TILES, HALVES, P, PAIR], BF16)
             nc.scalar.copy(
-                out=noise_turned[j][:].rearrange("p i u r e -> p i u (r e)"),
+                out=noise_turned[:].rearrange("p i u r e -> p i u (r e)"),
                 in_=noise_bank[j][:].bitcast(BF16),
             )
-            lr_grouped[j] = kept.tile([P, ROW_TILES, P, PACK], BF16, name="lr_grouped")
-            if j % 2 == 0:
-                nc.vector.tensor_copy(
-                    out=lr_grouped[j][:].bitcast(F32), in_=halves_together(lr_bank[j][:])
-                )
-            else:
-                nc.scalar.copy(out=lr_grouped[j][:].bitcast(F32), in_=halves_together(lr_bank[j][:]))
-
-        def by_example(columns):
-            return columns.rearrange("p i (m c) -> p i m c", c=EXAMPLE_COLS)
-
-        def along_samples(per_example):
-            return per_example.unsqueeze(1).unsqueeze(3).to_broadcast(
-                [P, ROW_TILES, EXAMPLES, EXAMPLE_COLS]
-            )
-
-        def scale_on_vector(j):
-            if not exists(j):
-                return
             shifted[j] = work.tile([P, ROW_TILES, PACK, P], F32, name="shifted")
-            examples = slice(j * EXAMPLES, (j + 1) * EXAMPLES)
-            for t in range(SCALAR_CODES, PACK):
-                u, e = divmod(t, PAIR)
-                nc.vector.tensor_tensor(
-                    out=by_example(shifted[j][:, :, t, :]),
-                    in0=by_example(noise_turned[j][:, :, u, :, e]),
-                    in1=along_samples(std[:, t, examples]),
-                    op=ALU.mult,
-                )
-
-        def shift_add(j):
-            if not exists(j):
-                return
-            examples = slice(j * EXAMPLES, (j + 1) * EXAMPLES)
-            for t in range(SCALAR_CODES, PACK):
-                u, e = divmod(t, PAIR)
-                nc.vector.tensor_tensor(
-                    out=by_example(shifted[j][:, :, t, :]),
-                    in0=by_example(shifted[j][:, :, t, :]),
-                    in1=along_samples(feat32[:, u, examples, e]),
-                    op=ALU.add,
-                )
             for m in range(EXAMPLES):
                 b = j * EXAMPLES + m
                 cols = slice(m * EXAMPLE_COLS, (m + 1) * EXAMPLE_COLS)
-                for t in range(SCALAR_CODES):
+                for t in range(PACK):
                     u, e = divmod(t, PAIR)
                     nc.scalar.activation(
                         out=shifted[j][:, :, t, cols],
-                        in_=noise_turned[j][:, :, u, cols, e],
+                        in_=noise_turned[:, :, u, cols, e],
                         func=ACT.Identity,
                         scale=std[:, t, b : b + 1],
                         bias=feat32[:, u, b, e : e + 1],
                     )
-            pre[j] = formed.tile([P, ROW_TILES, P, PACK], BF16, name="pre", align_bytes=64)
-            nc.gpsimd.tensor_tensor(
-                out=pre[j][:],
-                in0=shifted[j][:].rearrange("p i t r -> p i r t"),
-                in1=lr_grouped[j][:],
-                op=ALU.add,
-            )
+
+        def add_lr(j):
+            if not exists(j):
+                return
+            pre[j] = work.tile([P, ROW_TILES, P, PACK], BF16, name="pre", align_bytes=64)
+            for i in range(ROW_TILES):
+                nc.vector.tensor_tensor(
+                    out=pre[j][:, i].rearrange("p r (u e) -> p r u e", e=PAIR),
+                    in0=lr_bank[j][:, i].bitcast(BF16).rearrange("p u (r e) -> p r u e", e=PAIR),
+                    in1=shifted[j][:, i].rearrange("p (u e) r -> p r u e", e=PAIR),
+                    op=ALU.add,
+                )
 
         def quantise_block(j):
             if not exists(j):
@@ -309,13 +272,12 @@ def tile_hetxlhead_pa_kernel(
                 nc.sync.dma_start(out=out_blocks[j], in_=result[j][:])
 
         with tc.manual_schedule():
-            for j in range(-TURN_AHEAD, BLOCKS + 1):
-                turn(j + TURN_AHEAD)
+            for j in range(-SHIFT_AHEAD, BLOCKS + 1):
+                turn(j + SHIFT_AHEAD)
                 finish(j - 1, 0)
                 quantise_block(j)
                 multiply(j, 0)
-                keep_turned(j + TURN_AHEAD)
-                scale_on_vector(j + ADD_AHEAD)
+                shift(j + SHIFT_AHEAD)
                 finish(j - 1, 1)
                 multiply(j, 1)
-                shift_add(j + ADD_AHEAD)
+                add_lr(j + ADD_AHEAD)

@@ -28,6 +28,8 @@ EXAMPLE_COLS = P // EXAMPLES
 N_COLS = 512
 SHIFT_AHEAD = 2
 ADD_AHEAD = 1
+BANKS = ROW_TILES * (C // N_COLS)
+SCALAR_BANKS = 1
 MIN_SCALE = 1e-3
 INV_TEMPERATURE = 1.0 / 1.5
 
@@ -260,16 +262,29 @@ def tile_hetxlhead_pa_kernel(
                 result[j] = results.tile([P, ROW_TILES, C], F32, name="result")
             for h in range(C // N_COLS):
                 classes = slice(h * N_COLS, (h + 1) * N_COLS)
-                nc.vector.scalar_tensor_tensor(
-                    out=result[j][:, i, classes],
-                    in0=acc[j, i, h][:],
-                    scalar=INV_TEMPERATURE,
-                    in1=bias[:, classes],
-                    op0=ALU.mult,
-                    op1=ALU.add,
-                )
-            if i == ROW_TILES - 1:
-                nc.sync.dma_start(out=out_blocks[j], in_=result[j][:])
+                if i * (C // N_COLS) + h < BANKS - SCALAR_BANKS:
+                    nc.vector.scalar_tensor_tensor(
+                        out=result[j][:, i, classes],
+                        in0=acc[j, i, h][:],
+                        scalar=INV_TEMPERATURE,
+                        in1=bias[:, classes],
+                        op0=ALU.mult,
+                        op1=ALU.add,
+                    )
+                else:
+                    nc.scalar.activation(
+                        out=result[j][:, i, classes],
+                        in_=acc[j, i, h][:],
+                        func=ACT.Copy,
+                        scale=INV_TEMPERATURE,
+                    )
+                    nc.gpsimd.tensor_tensor(
+                        out=result[j][:, i, classes],
+                        in0=result[j][:, i, classes],
+                        in1=bias[:, classes],
+                        op=ALU.add,
+                    )
+            nc.sync.dma_start(out=out_blocks[j][:, i, :], in_=result[j][:, i, :])
 
         with tc.manual_schedule():
             for j in range(-SHIFT_AHEAD, BLOCKS + 1):
@@ -277,7 +292,7 @@ def tile_hetxlhead_pa_kernel(
                 finish(j - 1, 0)
                 quantise_block(j)
                 multiply(j, 0)
-                shift(j + SHIFT_AHEAD)
                 finish(j - 1, 1)
                 multiply(j, 1)
+                shift(j + SHIFT_AHEAD)
                 add_lr(j + ADD_AHEAD)

@@ -28,8 +28,8 @@ EXAMPLE_COLS = P // EXAMPLES
 N_COLS = 512
 SHIFT_AHEAD = 2
 ADD_AHEAD = 1
-BANKS = ROW_TILES * (C // N_COLS)
 SCALAR_BANKS = 1
+GPSIMD_EXAMPLES = 1
 MIN_SCALE = 1e-3
 INV_TEMPERATURE = 1.0 / 1.5
 
@@ -212,13 +212,23 @@ def tile_hetxlhead_pa_kernel(
                 cols = slice(m * EXAMPLE_COLS, (m + 1) * EXAMPLE_COLS)
                 for t in range(PACK):
                     u, e = divmod(t, PAIR)
-                    nc.scalar.activation(
-                        out=shifted[j][:, :, t, cols],
-                        in_=noise_turned[:, :, u, cols, e],
-                        func=ACT.Identity,
-                        scale=std[:, t, b : b + 1],
-                        bias=feat32[:, u, b, e : e + 1],
-                    )
+                    if m < EXAMPLES - GPSIMD_EXAMPLES:
+                        nc.scalar.activation(
+                            out=shifted[j][:, :, t, cols],
+                            in_=noise_turned[:, :, u, cols, e],
+                            func=ACT.Identity,
+                            scale=std[:, t, b : b + 1],
+                            bias=feat32[:, u, b, e : e + 1],
+                        )
+                    else:
+                        nc.gpsimd.tensor_scalar(
+                            out=shifted[j][:, :, t, cols],
+                            in0=noise_turned[:, :, u, cols, e],
+                            scalar1=std[:, t, b : b + 1],
+                            scalar2=feat32[:, u, b, e : e + 1],
+                            op0=ALU.mult,
+                            op1=ALU.add,
+                        )
 
         def add_lr(j):
             if not exists(j):
@@ -262,7 +272,7 @@ def tile_hetxlhead_pa_kernel(
                 result[j] = results.tile([P, ROW_TILES, C], F32, name="result")
             for h in range(C // N_COLS):
                 classes = slice(h * N_COLS, (h + 1) * N_COLS)
-                if i * (C // N_COLS) + h < BANKS - SCALAR_BANKS:
+                if i * (C // N_COLS) + h >= SCALAR_BANKS:
                     nc.vector.scalar_tensor_tensor(
                         out=result[j][:, i, classes],
                         in0=acc[j, i, h][:],

@@ -23,13 +23,12 @@ BLOCK_ROWS = ROW_TILES * P
 BLOCKS = B * S // BLOCK_ROWS
 BLOCKS_PER_LOAD = 4
 LOADS = BLOCKS // BLOCKS_PER_LOAD
-EXAMPLES = BLOCK_ROWS // S
-EXAMPLE_COLS = P // EXAMPLES
+EXAMPLES = P // S
 N_COLS = 512
 SHIFT_AHEAD = 2
 ADD_AHEAD = 1
+PRE_BUFS = 3 * ROW_TILES
 SCALAR_BANKS = 1
-GPSIMD_EXAMPLES = 1
 MIN_SCALE = 1e-3
 INV_TEMPERATURE = 1.0 / 1.5
 
@@ -60,13 +59,13 @@ def tile_hetxlhead_pa_kernel(
 ):
     nc = tc.nc
     noise_loads = noise_diag.rearrange("b s d -> (b s) d").rearrange(
-        "(l j p i) d -> l p j i d", j=BLOCKS_PER_LOAD, p=P, i=ROW_TILES
+        "(l j i p) d -> l p j i d", j=BLOCKS_PER_LOAD, p=P, i=ROW_TILES
     )
     lr_loads = lr_samples.rearrange("b s d -> (b s) d").rearrange(
-        "(l j p i) d -> l p j i d", j=BLOCKS_PER_LOAD, p=P, i=ROW_TILES
+        "(l j i p) d -> l p j i d", j=BLOCKS_PER_LOAD, p=P, i=ROW_TILES
     )
     out_blocks = out.rearrange("b s c -> (b s) c").rearrange(
-        "(j p i) c -> j p i c", p=P, i=ROW_TILES
+        "(j i p) c -> j p i c", p=P, i=ROW_TILES
     )
 
     with ExitStack() as ctx:
@@ -207,47 +206,39 @@ def tile_hetxlhead_pa_kernel(
                 in_=noise_bank[j][:].bitcast(BF16),
             )
             shifted[j] = work.tile([P, ROW_TILES, PACK, P], F32, name="shifted")
-            for m in range(EXAMPLES):
-                b = j * EXAMPLES + m
-                cols = slice(m * EXAMPLE_COLS, (m + 1) * EXAMPLE_COLS)
-                for t in range(PACK):
-                    u, e = divmod(t, PAIR)
-                    if m < EXAMPLES - GPSIMD_EXAMPLES:
+            for i in range(ROW_TILES):
+                for m in range(EXAMPLES):
+                    b = (j * ROW_TILES + i) * EXAMPLES + m
+                    samples = slice(m * S, (m + 1) * S)
+                    for t in range(PACK):
+                        u, e = divmod(t, PAIR)
                         nc.scalar.activation(
-                            out=shifted[j][:, :, t, cols],
-                            in_=noise_turned[:, :, u, cols, e],
+                            out=shifted[j][:, i, t, samples],
+                            in_=noise_turned[:, i, u, samples, e],
                             func=ACT.Identity,
                             scale=std[:, t, b : b + 1],
                             bias=feat32[:, u, b, e : e + 1],
                         )
-                    else:
-                        nc.gpsimd.tensor_scalar(
-                            out=shifted[j][:, :, t, cols],
-                            in0=noise_turned[:, :, u, cols, e],
-                            scalar1=std[:, t, b : b + 1],
-                            scalar2=feat32[:, u, b, e : e + 1],
-                            op0=ALU.mult,
-                            op1=ALU.add,
-                        )
 
-        def add_lr(j):
+        def add_lr(j, i):
             if not exists(j):
                 return
-            pre[j] = work.tile([P, ROW_TILES, P, PACK], BF16, name="pre", align_bytes=64)
-            for i in range(ROW_TILES):
-                nc.vector.tensor_tensor(
-                    out=pre[j][:, i].rearrange("p r (u e) -> p r u e", e=PAIR),
-                    in0=lr_bank[j][:, i].bitcast(BF16).rearrange("p u (r e) -> p r u e", e=PAIR),
-                    in1=shifted[j][:, i].rearrange("p (u e) r -> p r u e", e=PAIR),
-                    op=ALU.add,
-                )
+            pre[j, i] = work.tile([P, 1, P, PACK], BF16, name="pre", bufs=PRE_BUFS, align_bytes=64)
+            nc.vector.tensor_tensor(
+                out=pre[j, i][:, 0].rearrange("p r (u e) -> p r u e", e=PAIR),
+                in0=lr_bank[j][:, i].bitcast(BF16).rearrange("p u (r e) -> p r u e", e=PAIR),
+                in1=shifted[j][:, i].rearrange("p (u e) r -> p r u e", e=PAIR),
+                op=ALU.add,
+            )
 
-        def quantise_block(j):
+        def quantise_tile(j, i):
             if not exists(j):
                 return
-            pre_codes[j] = work.tile([P, BLOCK_ROWS], U32, name="pre_codes", align_bytes=64)
-            pre_scales[j] = work.tile([P, BLOCK_ROWS], U8, name="pre_scales", align_bytes=64)
-            quantise(nc, pre_codes[j][:], pre_scales[j][:], pre[j][:])
+            pre_codes[j, i] = work.tile([P, P], U32, name="pre_codes", bufs=PRE_BUFS, align_bytes=64)
+            pre_scales[j, i] = work.tile(
+                [P, P], U8, name="pre_scales", bufs=PRE_BUFS, align_bytes=64
+            )
+            quantise(nc, pre_codes[j, i][:], pre_scales[j, i][:], pre[j, i][:])
 
         def multiply(j, i):
             if not exists(j):
@@ -257,8 +248,8 @@ def tile_hetxlhead_pa_kernel(
                 acc[j, i, h] = sums.tile([P, N_COLS], F32, name="acc", tag="sums")
                 nc.tensor.matmul_mx(
                     out=acc[j, i, h][:],
-                    lhsT=pre_codes[j][:, i * P : (i + 1) * P].bitcast(FP8X4),
-                    lhsT_scale=pre_scales[j][:, i * P : (i + 1) * P],
+                    lhsT=pre_codes[j, i][:].bitcast(FP8X4),
+                    lhsT_scale=pre_scales[j, i][:],
                     rhs=wc_codes[:, classes].bitcast(FP8X4),
                     rhs_scale=wc_scales[:, classes],
                     start=True,
@@ -299,10 +290,10 @@ def tile_hetxlhead_pa_kernel(
         with tc.manual_schedule():
             for j in range(-SHIFT_AHEAD, BLOCKS + 1):
                 turn(j + SHIFT_AHEAD)
-                finish(j - 1, 0)
-                quantise_block(j)
-                multiply(j, 0)
-                finish(j - 1, 1)
-                multiply(j, 1)
+                for i in range(ROW_TILES):
+                    finish(j - 1, i)
+                    quantise_tile(j, i)
+                    multiply(j, i)
                 shift(j + SHIFT_AHEAD)
-                add_lr(j + ADD_AHEAD)
+                for i in range(ROW_TILES):
+                    add_lr(j + ADD_AHEAD, i)

from contextlib import ExitStack

import concourse.mybir as mybir
from concourse.masks import make_identity

F32 = mybir.dt.float32
BF16 = mybir.dt.bfloat16
U32 = mybir.dt.uint32
U8 = mybir.dt.uint8
FP8X4 = mybir.dt.float8_e4m3fn_x4
ACT = mybir.ActivationFunctionType
ALU = mybir.AluOpType

P = 128
PAIR = 2
HALVES = 2
PACK = HALVES * PAIR
B, S, D, C = 128, 32, 512, 1024
assert D == P * PACK

ROW_TILES = 2
BLOCK_ROWS = ROW_TILES * P
BLOCKS = B * S // BLOCK_ROWS
BLOCKS_PER_LOAD = 4
LOADS = BLOCKS // BLOCKS_PER_LOAD
EXAMPLES = P // S
N_COLS = 512
SHIFT_AHEAD = 2
ADD_AHEAD = 1
PRE_BUFS = 3 * ROW_TILES
SCALAR_BANKS = 1
MIN_SCALE = 1e-3
INV_TEMPERATURE = 1.0 / 1.5

FLOPS = 2 * B * S * D * C + 2 * B * D * D


def turn_row_tiles(nc, bank, rows, identity):
    for i in range(rows.shape[1]):
        words = rows[:, i, :].bitcast(F32)
        for u in range(HALVES):
            nc.tensor.transpose(bank[:, i, u, :], words[:, u * P : (u + 1) * P], identity)


def halves_together(bank):
    return bank.rearrange("p i u r -> p i r u")


def quantise(nc, codes, scales, grouped):
    nc.vector.quantize_mx(
        out=codes.bitcast(FP8X4),
        scales=scales,
        in_=grouped.rearrange("p i r t -> p (i r t)"),
    )


def tile_hetxlhead_pa_kernel(
    tc, features, W_diag, b_diag, W_cls, b_cls, noise_diag, lr_samples, out
):
    nc = tc.nc
    noise_loads = noise_diag.rearrange("b s d -> (b s) d").rearrange(
        "(l j i p) d -> l p j i d", j=BLOCKS_PER_LOAD, p=P, i=ROW_TILES
    )
    lr_loads = lr_samples.rearrange("b s d -> (b s) d").rearrange(
        "(l j i p) d -> l p j i d", j=BLOCKS_PER_LOAD, p=P, i=ROW_TILES
    )
    out_blocks = out.rearrange("b s c -> (b s) c").rearrange(
        "(j i p) c -> j p i c", p=P, i=ROW_TILES
    )

    with ExitStack() as ctx:
        keep = ctx.enter_context(tc.tile_pool(name="keep", bufs=1))
        work = ctx.enter_context(tc.tile_pool(name="work", bufs=3))
        results = ctx.enter_context(tc.tile_pool(name="results", bufs=3))
        turned = ctx.enter_context(tc.psum_pool(name="turned", bufs=4))
        sums = ctx.enter_context(tc.psum_pool(name="sums", bufs=4))

        def turn_weight(grouped, rows):
            for g in range(rows.shape[1] // ROW_TILES):
                pair = slice(g * ROW_TILES, (g + 1) * ROW_TILES)
                bank = turned.tile([P, ROW_TILES, HALVES, P], F32, tag="turned")
                turn_row_tiles(nc, bank[:], rows[:, pair], identity[:])
                if g % 2 == 0:
                    nc.vector.tensor_copy(
                        out=grouped[:, pair].bitcast(F32), in_=halves_together(bank[:])
                    )
                else:
                    nc.scalar.copy(out=grouped[:, pair].bitcast(F32), in_=halves_together(bank[:]))

        identity = keep.tile([P, P], F32)
        make_identity(nc, identity[:])
        one = keep.tile([P, 1], F32)
        nc.vector.memset(one[:], 1.0)
        warm = keep.tile([P, 1], F32)
        nc.scalar.activation(out=warm[:], in_=one[:], func=ACT.Exp)
        bd_rows = keep.tile([P, 1, PAIR * P], BF16)
        nc.vector.memset(bd_rows[:], 0.0)

        nc.sync.dma_start(
            out=bd_rows[0:HALVES, 0, :], in_=b_diag.rearrange("(u w) -> u w", u=HALVES)
        )
        feat_rows = keep.tile([P, 1, D], BF16)
        nc.sync.dma_start(out=feat_rows[:, 0, :], in_=features)
        wd_rows = keep.tile([P, PACK, D], BF16)
        nc.sync.dma_start(
            out=wd_rows[:].rearrange("r (u e) k -> r u e k", u=HALVES),
            in_=W_diag.rearrange("(u r e) k -> r u e k", u=HALVES, e=PAIR),
        )
        noise_rows = []
        lr_rows = []
        wc_rows = keep.tile([P, C // P, D], BF16)
        bc_rows = keep.tile([P, C], BF16)
        for l in range(LOADS):
            noise_rows.append(
                keep.tile([P, BLOCKS_PER_LOAD, ROW_TILES, D], BF16, name="noise_rows%d" % l)
            )
            nc.sync.dma_start(out=noise_rows[l][:], in_=noise_loads[l])
            lr_rows.append(
                keep.tile([P, BLOCKS_PER_LOAD, ROW_TILES, D], BF16, name="lr_rows%d" % l)
            )
            nc.sync.dma_start(out=lr_rows[l][:], in_=lr_loads[l])
            if l == 0:
                nc.sync.dma_start(out=wc_rows[:], in_=W_cls.rearrange("(i r) k -> r i k", r=P))
                nc.sync.dma_start(out=bc_rows[:], in_=b_cls.partition_broadcast(P))

        head_bank = turned.tile([P, ROW_TILES, HALVES, P], F32, tag="turned")
        turn_row_tiles(nc, head_bank[:, 0:1], feat_rows[:], identity[:])
        nc.tensor.transpose(head_bank[:, 1, 0, :], bd_rows[:, 0, :].bitcast(F32), identity[:])
        feat = keep.tile([P, 1, B, PACK], BF16, align_bytes=64)
        nc.vector.tensor_copy(out=feat[:].bitcast(F32), in_=halves_together(head_bank[:, 0:1]))
        feat32 = keep.tile([P, HALVES, B, PAIR], F32)
        nc.vector.tensor_copy(
            out=feat32[:].rearrange("p u b e -> p u (b e)"), in_=head_bank[:, 0].bitcast(BF16)
        )
        bd = keep.tile([P, PACK], F32)
        nc.vector.tensor_copy(out=bd[:], in_=head_bank[:, 1, 0, 0:HALVES].bitcast(BF16))

        wd = keep.tile([P, PACK, P, PACK], BF16, align_bytes=64)
        turn_weight(wd, wd_rows)
        feat_codes = keep.tile([P, B], U32, align_bytes=64)
        feat_scales = keep.tile([P, B], U8, align_bytes=64)
        quantise(nc, feat_codes[:], feat_scales[:], feat[:])
        wd_codes = keep.tile([P, D], U32, align_bytes=64)
        wd_scales = keep.tile([P, D], U8, align_bytes=64)
        quantise(nc, wd_codes[:], wd_scales[:], wd[:])

        z = sums.tile([P, PACK, B], F32, tag="sums")
        for t in range(PACK):
            nc.tensor.matmul_mx(
                out=z[:, t, :],
                lhsT=wd_codes[:, t * P : (t + 1) * P].bitcast(FP8X4),
                lhsT_scale=wd_scales[:, t * P : (t + 1) * P],
                rhs=feat_codes[:].bitcast(FP8X4),
                rhs_scale=feat_scales[:],
                start=True,
                stop=True,
            )
        v = keep.tile([P, PACK, B], F32)
        nc.vector.tensor_tensor(
            out=v[:], in0=z[:], in1=bd[:].unsqueeze(2).to_broadcast([P, PACK, B]), op=ALU.add
        )
        magnitude = keep.tile([P, PACK, B], F32)
        nc.scalar.activation(out=magnitude[:], in_=v[:], func=ACT.Abs)
        decay = keep.tile([P, PACK, B], F32)
        nc.scalar.activation(out=decay[:], in_=magnitude[:], func=ACT.Exp, scale=-1.0)
        log_term = keep.tile([P, PACK, B], F32)
        nc.scalar.activation(out=log_term[:], in_=decay[:], func=ACT.Ln, bias=one[:])
        ramp = keep.tile([P, PACK, B], F32)
        nc.vector.tensor_scalar(
            out=ramp[:], in0=v[:], scalar1=0.0, scalar2=MIN_SCALE, op0=ALU.max, op1=ALU.add
        )
        std = keep.tile([P, PACK, B], F32)
        nc.vector.tensor_tensor(out=std[:], in0=log_term[:], in1=ramp[:], op=ALU.add)

        wc = keep.tile([P, C // P, P, PACK], BF16, align_bytes=64)
        turn_weight(wc, wc_rows)
        wc_codes = keep.tile([P, C], U32, align_bytes=64)
        wc_scales = keep.tile([P, C], U8, align_bytes=64)
        quantise(nc, wc_codes[:], wc_scales[:], wc[:])
        bias = keep.tile([P, C], F32)
        nc.vector.tensor_scalar_mul(out=bias[:], in0=bc_rows[:], scalar1=INV_TEMPERATURE)

        noise_bank, lr_bank, shifted = {}, {}, {}
        pre, pre_codes, pre_scales, acc, result = {}, {}, {}, {}, {}

        def exists(j):
            return 0 <= j < BLOCKS

        def turn(j):
            if not exists(j):
                return
            l, k = divmod(j, BLOCKS_PER_LOAD)
            noise_bank[j] = turned.tile(
                [P, ROW_TILES, HALVES, P], F32, name="noise_bank", tag="turned"
            )
            turn_row_tiles(nc, noise_bank[j][:], noise_rows[l][:, k], identity[:])
            lr_bank[j] = turned.tile([P, ROW_TILES, HALVES, P], F32, name="lr_bank", tag="turned")
            turn_row_tiles(nc, lr_bank[j][:], lr_rows[l][:, k], identity[:])

        def shift(j):
            if not exists(j):
                return
            noise_turned = work.tile([P, ROW_TILES, HALVES, P, PAIR], BF16)
            nc.scalar.copy(
                out=noise_turned[:].rearrange("p i u r e -> p i u (r e)"),
                in_=noise_bank[j][:].bitcast(BF16),
            )
            shifted[j] = work.tile([P, ROW_TILES, PACK, P], F32, name="shifted")
            for i in range(ROW_TILES):
                for m in range(EXAMPLES):
                    b = (j * ROW_TILES + i) * EXAMPLES + m
                    samples = slice(m * S, (m + 1) * S)
                    for t in range(PACK):
                        u, e = divmod(t, PAIR)
                        nc.scalar.activation(
                            out=shifted[j][:, i, t, samples],
                            in_=noise_turned[:, i, u, samples, e],
                            func=ACT.Identity,
                            scale=std[:, t, b : b + 1],
                            bias=feat32[:, u, b, e : e + 1],
                        )

        def add_lr(j, i):
            if not exists(j):
                return
            pre[j, i] = work.tile([P, 1, P, PACK], BF16, name="pre", bufs=PRE_BUFS, align_bytes=64)
            nc.vector.tensor_tensor(
                out=pre[j, i][:, 0].rearrange("p r (u e) -> p r u e", e=PAIR),
                in0=lr_bank[j][:, i].bitcast(BF16).rearrange("p u (r e) -> p r u e", e=PAIR),
                in1=shifted[j][:, i].rearrange("p (u e) r -> p r u e", e=PAIR),
                op=ALU.add,
            )

        def quantise_tile(j, i):
            if not exists(j):
                return
            pre_codes[j, i] = work.tile([P, P], U32, name="pre_codes", bufs=PRE_BUFS, align_bytes=64)
            pre_scales[j, i] = work.tile(
                [P, P], U8, name="pre_scales", bufs=PRE_BUFS, align_bytes=64
            )
            quantise(nc, pre_codes[j, i][:], pre_scales[j, i][:], pre[j, i][:])

        def multiply(j, i):
            if not exists(j):
                return
            for h in range(C // N_COLS):
                classes = slice(h * N_COLS, (h + 1) * N_COLS)
                acc[j, i, h] = sums.tile([P, N_COLS], F32, name="acc", tag="sums")
                nc.tensor.matmul_mx(
                    out=acc[j, i, h][:],
                    lhsT=pre_codes[j, i][:].bitcast(FP8X4),
                    lhsT_scale=pre_scales[j, i][:],
                    rhs=wc_codes[:, classes].bitcast(FP8X4),
                    rhs_scale=wc_scales[:, classes],
                    start=True,
                    stop=True,
                )

        def finish(j, i):
            if not exists(j):
                return
            if i == 0:
                result[j] = results.tile([P, ROW_TILES, C], F32, name="result")
            for h in range(C // N_COLS):
                classes = slice(h * N_COLS, (h + 1) * N_COLS)
                if i * (C // N_COLS) + h >= SCALAR_BANKS:
                    nc.vector.scalar_tensor_tensor(
                        out=result[j][:, i, classes],
                        in0=acc[j, i, h][:],
                        scalar=INV_TEMPERATURE,
                        in1=bias[:, classes],
                        op0=ALU.mult,
                        op1=ALU.add,
                    )
                else:
                    nc.scalar.activation(
                        out=result[j][:, i, classes],
                        in_=acc[j, i, h][:],
                        func=ACT.Copy,
                        scale=INV_TEMPERATURE,
                    )
                    nc.gpsimd.tensor_tensor(
                        out=result[j][:, i, classes],
                        in0=result[j][:, i, classes],
                        in1=bias[:, classes],
                        op=ALU.add,
                    )
            nc.sync.dma_start(out=out_blocks[j][:, i, :], in_=result[j][:, i, :])

        with tc.manual_schedule():
            for j in range(-SHIFT_AHEAD, BLOCKS + 1):
                turn(j + SHIFT_AHEAD)
                for i in range(ROW_TILES):
                    finish(j - 1, i)
                    quantise_tile(j, i)
                    multiply(j, i)
                shift(j + SHIFT_AHEAD)
                for i in range(ROW_TILES):
                    add_lr(j + ADD_AHEAD, i)
